import numpy as np
import ml_dtypes


def mxq(x, axis, fmt="e4m3"):
    dtype, down = {"e4m3": (ml_dtypes.float8_e4m3fn, 7), "e5m2": (ml_dtypes.float8_e5m2, 14)}[fmt]
    v = np.moveaxis(np.asarray(x, np.float32).astype(ml_dtypes.bfloat16).astype(np.float64), axis, -1)
    blocks = v.reshape(v.shape[:-1] + (-1, 32))
    amax = np.abs(blocks).max(-1, keepdims=True)
    byte = np.maximum(np.where(amax > 0, np.frexp(amax)[1] - 1 + 127, 0) - down, 1)
    scale = np.exp2(byte - 127.0)
    codes = (blocks / scale).astype(np.float32).astype(dtype).astype(np.float64)
    return np.moveaxis((codes * scale).reshape(v.shape), -1, axis)


WIDE = False


def mx_kscale(k):
    if not WIDE:
        return np.ones(k)
    levels = np.array([10, -10, 5, -5, 0])
    a = np.random.permutation(np.resize(levels, k // 512 * 4)).reshape(k // 512, 4)
    idx = np.arange(k)
    return np.exp2(a[idx // 512, idx % 128 // 32])


BF16 = ml_dtypes.bfloat16


def bf(x):
    return np.asarray(x, np.float32).astype(BF16)


def f64(x):
    return np.asarray(x).astype(np.float64)


B, N, D, H, W = 1, 128, 1024, 16, 16
HD = D // H
DF = N * HD // W


def setup_inputs():
    s = mx_kscale(D)
    u = mx_kscale(D)
    r = np.concatenate([u, 1.0 / u])
    return {"x": bf(np.random.standard_normal((B, N, D)) * s),
            "Wqk": bf(np.random.standard_normal((2 * D, D)) * 0.8 / np.sqrt(D) * r[:, None] / s)}


def reference(x, Wqk):
    qk = mxq(f64(x), 2, "e4m3") @ mxq(f64(Wqk), 1, "e4m3").T
    qk = qk.reshape(B, N, 2, H, HD).transpose(2, 0, 3, 1, 4)
    q = (qk[0] * HD ** -0.5).reshape(B * H, W, DF)
    k = qk[1].reshape(B * H, W, DF)
    s = mxq(q, 2, "e4m3") @ mxq(k, 2, "e4m3").transpose(0, 2, 1)
    e = np.exp(s - s.max(-1, keepdims=True))
    return e / e.sum(-1, keepdims=True)

@@ -1,0 +1,210 @@
+from contextlib import ExitStack
+
+import concourse.mybir as mybir
+from concourse.masks import make_identity
+
+F32 = mybir.dt.float32
+BF16 = mybir.dt.bfloat16
+U32 = mybir.dt.uint32
+U8 = mybir.dt.uint8
+FP8X4 = mybir.dt.float8_e4m3fn_x4
+ALU = mybir.AluOpType
+ACT = mybir.ActivationFunctionType
+AXIS_X = mybir.AxisListType.X
+
+P = 128
+PACK = 4
+TOKENS = 128
+MODEL = 1024
+HEADS = 16
+HEAD_DIM = 64
+WINDOW_ROWS = 16
+ROW_TOKENS = TOKENS // WINDOW_ROWS
+
+PASSES = MODEL // (P * PACK)
+HALVES = 2
+BLOCKS = 2 * HEADS * HEAD_DIM // P
+GROUP = 4
+GROUPS = BLOCKS // GROUP
+QUERY_GROUPS = GROUPS // 2
+PAIRS = HEADS // 2
+TOKEN_PASSES = ROW_TOKENS // PACK
+COLS = WINDOW_ROWS * PACK
+
+FLOPS = 2 * TOKENS * MODEL * 2 * MODEL + HEADS * 2 * WINDOW_ROWS * WINDOW_ROWS * ROW_TOKENS * HEAD_DIM
+
+
+def flip_rows(nc, banks, rows, order):
+    words = rows[:].bitcast(F32)
+    flipped = banks.tile([P, PASSES, HALVES, P], F32, tag="flipped")
+    for g in range(PASSES):
+        for u in range(HALVES):
+            first = (g * HALVES + u) * P
+            nc.tensor.transpose(flipped[:, g, u, :], words[:, first : first + P], order[:])
+    return flipped
+
+
+def tile_slidingwindowattention_pa_s_kernel(tc, x, Wqk, out):
+    nc = tc.nc
+    with ExitStack() as ctx:
+        consts = ctx.enter_context(tc.tile_pool(name="consts", bufs=1))
+        rows_pool = ctx.enter_context(tc.tile_pool(name="rows", bufs=BLOCKS))
+        packed = ctx.enter_context(tc.tile_pool(name="packed", bufs=BLOCKS))
+        keep = ctx.enter_context(tc.tile_pool(name="keep", bufs=1))
+        banks = ctx.enter_context(tc.psum_pool(name="banks", bufs=4))
+        proj_banks = ctx.enter_context(tc.psum_pool(name="proj_banks", bufs=3))
+        score_banks = ctx.enter_context(tc.psum_pool(name="score_banks", bufs=1))
+
+        x_rows = consts.tile([P, MODEL], BF16)
+        nc.sync.dma_start(out=x_rows[:], in_=x.flatten_outer_dims())
+        w_rows = []
+        for b in range(BLOCKS):
+            block_rows = rows_pool.tile([P, MODEL], BF16)
+            nc.sync.dma_start(out=block_rows[:], in_=Wqk[b * P : (b + 1) * P, :])
+            w_rows.append(block_rows)
+
+        identity = consts.tile([P, P], F32)
+        make_identity(nc, identity[:])
+        token_order = consts.tile([P, P], F32)
+        nc.vector.tensor_copy(
+            out=token_order[:].rearrange("p (r w t) -> p r w t", r=TOKEN_PASSES, w=WINDOW_ROWS),
+            in_=identity[:].rearrange("p (w r t) -> p r w t", w=WINDOW_ROWS, r=TOKEN_PASSES),
+        )
+        warm = consts.tile([P, 1], F32)
+        nc.vector.memset(warm[:], 0.0)
+        nc.scalar.activation(out=warm[:], in_=warm[:], func=ACT.Exp)
+        own_pair = consts.tile([P, QUERY_GROUPS, PAIRS, WINDOW_ROWS], F32)
+        nc.vector.memset(own_pair[:], 0.0)
+        for a in range(QUERY_GROUPS):
+            for i in range(GROUP):
+                nc.vector.memset(own_pair[32 * i : 32 * i + 32, a, GROUP * a + i, :], 1.0)
+        q_grouped = keep.tile(
+            [P, QUERY_GROUPS, TOKEN_PASSES, GROUP, 2, COLS], BF16, align_bytes=64
+        )
+        nc.vector.memset(q_grouped[:], 0.0)
+        k_grouped = keep.tile([P, TOKEN_PASSES, PAIRS, COLS], BF16, align_bytes=64)
+
+        x_flipped = flip_rows(nc, banks, x_rows, token_order)
+        x_grouped = keep.tile([P, PASSES, TOKENS, PACK], BF16, align_bytes=64)
+        nc.scalar.copy(
+            out=x_grouped[:].bitcast(F32), in_=x_flipped[:].rearrange("p g u n -> p g n u")
+        )
+        x_codes = keep.tile([P, PASSES, TOKENS], U32, align_bytes=64)
+        x_scales = keep.tile([P, PASSES, TOKENS], U8, align_bytes=64)
+        nc.vector.quantize_mx(
+            out=x_codes[:].rearrange("p g n -> p (g n)").bitcast(FP8X4),
+            scales=x_scales[:].rearrange("p g n -> p (g n)"),
+            in_=x_grouped[:].rearrange("p g n t -> p (g n t)"),
+        )
+
+        w_codes = []
+        w_scales = []
+
+        def quantise_group(c):
+            for i in range(GROUP):
+                flipped = flip_rows(nc, banks, w_rows[GROUP * c + i], identity)
+                grouped = packed.tile([P, PASSES, P, PACK], BF16, align_bytes=64)
+                copy = nc.vector.tensor_copy if i == 2 else nc.scalar.copy
+                copy(out=grouped[:].bitcast(F32), in_=flipped[:].rearrange("p g u m -> p g m u"))
+                codes = packed.tile([P, PASSES, P], U32, align_bytes=64)
+                scales = packed.tile([P, PASSES, P], U8, align_bytes=64)
+                nc.vector.quantize_mx(
+                    out=codes[:].rearrange("p g m -> p (g m)").bitcast(FP8X4),
+                    scales=scales[:].rearrange("p g m -> p (g m)"),
+                    in_=grouped[:].rearrange("p g m t -> p (g m t)"),
+                )
+                w_codes.append(codes)
+                w_scales.append(scales)
+
+        def project_group(c):
+            proj = proj_banks.tile([P, GROUP, TOKEN_PASSES, COLS], F32)
+            for i in range(GROUP):
+                b = GROUP * c + i
+                for g in range(PASSES):
+                    nc.tensor.matmul_mx(
+                        out=proj[:, i, :, :].rearrange("p r n -> p (r n)"),
+                        lhsT=w_codes[b][:, g, :].bitcast(FP8X4),
+                        lhsT_scale=w_scales[b][:, g, :],
+                        rhs=x_codes[:, g, :].bitcast(FP8X4),
+                        rhs_scale=x_scales[:, g, :],
+                        start=(g == 0),
+                        stop=(g == PASSES - 1),
+                    )
+            by_pass = proj[:].rearrange("p i r n -> p r i n")
+            if c < QUERY_GROUPS:
+                for e in range(2):
+                    head = slice(HEAD_DIM * e, HEAD_DIM * (e + 1))
+                    nc.scalar.activation(
+                        out=q_grouped[head, c, :, :, e, :],
+                        in_=by_pass[head],
+                        func=ACT.Copy,
+                        scale=HEAD_DIM**-0.5,
+                    )
+            else:
+                first = GROUP * (c - QUERY_GROUPS)
+                nc.vector.tensor_copy(out=k_grouped[:, :, first : first + GROUP, :], in_=by_pass)
+
+        quantise_group(0)
+        for c in range(GROUPS):
+            if c + 1 < GROUPS:
+                quantise_group(c + 1)
+            project_group(c)
+
+        q_codes = keep.tile([P, QUERY_GROUPS, TOKEN_PASSES, P], U32, align_bytes=64)
+        q_scales = keep.tile([P, QUERY_GROUPS, TOKEN_PASSES, P], U8, align_bytes=64)
+        nc.vector.quantize_mx(
+            out=q_codes[:].rearrange("p a r m -> p (a r m)").bitcast(FP8X4),
+            scales=q_scales[:].rearrange("p a r m -> p (a r m)"),
+            in_=q_grouped[:].rearrange("p a r i e n -> p (a r i e n)"),
+        )
+        k_codes = keep.tile([P, TOKEN_PASSES, P], U32, align_bytes=64)
+        k_scales = keep.tile([P, TOKEN_PASSES, P], U8, align_bytes=64)
+        nc.vector.quantize_mx(
+            out=k_codes[:].rearrange("p r n -> p (r n)").bitcast(FP8X4),
+            scales=k_scales[:].rearrange("p r n -> p (r n)"),
+            in_=k_grouped[:].rearrange("p r c n -> p (r c n)"),
+        )
+
+        all_pairs = score_banks.tile([P, QUERY_GROUPS, PAIRS, WINDOW_ROWS], F32)
+        for a in range(QUERY_GROUPS):
+            for r in range(TOKEN_PASSES):
+                nc.tensor.matmul_mx(
+                    out=all_pairs[:, a, :, :].rearrange("p c v -> p (c v)"),
+                    lhsT=q_codes[:, a, r, :].bitcast(FP8X4),
+                    lhsT_scale=q_scales[:, a, r, :],
+                    rhs=k_codes[:, r, :].bitcast(FP8X4),
+                    rhs_scale=k_scales[:, r, :],
+                    start=(r == 0),
+                    stop=(r == TOKEN_PASSES - 1),
+                )
+
+        picked = keep.tile([P, QUERY_GROUPS, PAIRS, WINDOW_ROWS], F32)
+        nc.vector.tensor_tensor(out=picked[:], in0=all_pairs[:], in1=own_pair[:], op=ALU.mult)
+        scores = keep.tile([P, QUERY_GROUPS, WINDOW_ROWS], F32)
+        nc.vector.tensor_reduce(
+            out=scores[:], in_=picked[:].rearrange("p a c v -> p a v c"), axis=AXIS_X, op=ALU.add
+        )
+
+        neg_max = keep.tile([P, QUERY_GROUPS], F32)
+        nc.vector.tensor_reduce(out=neg_max[:], in_=scores[:], axis=AXIS_X, op=ALU.max, negate=True)
+        weights = keep.tile([P, QUERY_GROUPS, WINDOW_ROWS], F32)
+        row_sum = keep.tile([P, QUERY_GROUPS], F32)
+        for a in range(QUERY_GROUPS):
+            nc.scalar.activation(
+                out=weights[:, a, :],
+                in_=scores[:, a, :],
+                func=ACT.Exp,
+                bias=neg_max[:, a : a + 1],
+                accum_out=row_sum[:, a : a + 1],
+            )
+        inverse = keep.tile([P, QUERY_GROUPS], F32)
+        nc.vector.reciprocal(out=inverse[:], in_=row_sum[:])
+        nc.vector.tensor_tensor(
+            out=weights[:],
+            in0=weights[:],
+            in1=inverse[:].unsqueeze(2).to_broadcast([P, QUERY_GROUPS, WINDOW_ROWS]),
+            op=ALU.mult,
+        )
+        nc.sync.dma_start(
+            out=out.rearrange("(a h) w v -> (h w) a v", a=QUERY_GROUPS), in_=weights[:]
+        )

@@ -7,6 +7,7 @@ F32 = mybir.dt.float32
 BF16 = mybir.dt.bfloat16
 U32 = mybir.dt.uint32
 U8 = mybir.dt.uint8
+I32 = mybir.dt.int32
 FP8X4 = mybir.dt.float8_e4m3fn_x4
 ALU = mybir.AluOpType
 ACT = mybir.ActivationFunctionType
@@ -30,6 +31,8 @@ QUERY_GROUPS = GROUPS // 2
 PAIRS = HEADS // 2
 TOKEN_PASSES = ROW_TOKENS // PACK
 COLS = WINDOW_ROWS * PACK
+BANK = 512
+WARM_PASSES = 6
 
 FLOPS = 2 * TOKENS * MODEL * 2 * MODEL + HEADS * 2 * WINDOW_ROWS * WINDOW_ROWS * ROW_TOKENS * HEAD_DIM
 
@@ -62,6 +65,25 @@ def tile_slidingwindowattention_pa_s_kernel(tc, x, Wqk, out):
             block_rows = rows_pool.tile([P, MODEL], BF16)
             nc.sync.dma_start(out=block_rows[:], in_=Wqk[b * P : (b + 1) * P, :])
             w_rows.append(block_rows)
+
+        zero_values = consts.tile([P, BANK * PACK], BF16, align_bytes=64)
+        zero_codes = consts.tile([P, BANK], U32, align_bytes=64)
+        zero_scales = consts.tile([P, BANK], U8, align_bytes=64)
+        nc.vector.memset(zero_values[:].bitcast(I32), 0)
+        nc.vector.quantize_mx(
+            out=zero_codes[:].bitcast(FP8X4), scales=zero_scales[:], in_=zero_values[:]
+        )
+        zero_bank = score_banks.tile([P, BANK], F32, tag="scores")
+        for n in range(WARM_PASSES):
+            nc.tensor.matmul_mx(
+                out=zero_bank[:],
+                lhsT=zero_codes[:, :P].bitcast(FP8X4),
+                lhsT_scale=zero_scales[:, :P],
+                rhs=zero_codes[:].bitcast(FP8X4),
+                rhs_scale=zero_scales[:],
+                start=True,
+                stop=True,
+            )
 
         identity = consts.tile([P, P], F32)
         make_identity(nc, identity[:])
@@ -165,7 +187,7 @@ def tile_slidingwindowattention_pa_s_kernel(tc, x, Wqk, out):
             in_=k_grouped[:].rearrange("p r c n -> p (r c n)"),
         )
 
-        all_pairs = score_banks.tile([P, QUERY_GROUPS, PAIRS, WINDOW_ROWS], F32)
+        all_pairs = score_banks.tile([P, QUERY_GROUPS, PAIRS, WINDOW_ROWS], F32, tag="scores")
         for a in range(QUERY_GROUPS):
             for r in range(TOKEN_PASSES):
                 nc.tensor.matmul_mx(

@@ -5,9 +5,9 @@ from concourse.masks import make_identity
 
 F32 = mybir.dt.float32
 BF16 = mybir.dt.bfloat16
+I32 = mybir.dt.int32
 U32 = mybir.dt.uint32
 U8 = mybir.dt.uint8
-I32 = mybir.dt.int32
 FP8X4 = mybir.dt.float8_e4m3fn_x4
 ALU = mybir.AluOpType
 ACT = mybir.ActivationFunctionType
@@ -24,15 +24,14 @@ ROW_TOKENS = TOKENS // WINDOW_ROWS
 
 PASSES = MODEL // (P * PACK)
 HALVES = 2
-BLOCKS = 2 * HEADS * HEAD_DIM // P
-GROUP = 4
-GROUPS = BLOCKS // GROUP
-QUERY_GROUPS = GROUPS // 2
 PAIRS = HEADS // 2
 TOKEN_PASSES = ROW_TOKENS // PACK
 COLS = WINDOW_ROWS * PACK
-BANK = 512
-WARM_PASSES = 6
+QUADRANT = 32
+GROUP = P // QUADRANT
+GROUPS = PAIRS // GROUP
+RUN = 2
+STEPS = 2 * PAIRS // RUN
 
 FLOPS = 2 * TOKENS * MODEL * 2 * MODEL + HEADS * 2 * WINDOW_ROWS * WINDOW_ROWS * ROW_TOKENS * HEAD_DIM
 
@@ -47,44 +46,39 @@ def flip_rows(nc, banks, rows, order):
     return flipped
 
 
+def quantise(nc, pool, name, grouped, columns):
+    codes = pool.tile([P, columns], U32, align_bytes=64, tag=name + "_codes")
+    scales = pool.tile([P, columns], U8, align_bytes=64, tag=name + "_scales")
+    nc.vector.quantize_mx(out=codes[:].bitcast(FP8X4), scales=scales[:], in_=grouped)
+    return codes, scales
+
+
 def tile_slidingwindowattention_pa_s_kernel(tc, x, Wqk, out):
     nc = tc.nc
     with ExitStack() as ctx:
+        ctx.enter_context(tc.manual_schedule())
         consts = ctx.enter_context(tc.tile_pool(name="consts", bufs=1))
-        rows_pool = ctx.enter_context(tc.tile_pool(name="rows", bufs=BLOCKS))
-        packed = ctx.enter_context(tc.tile_pool(name="packed", bufs=BLOCKS))
-        keep = ctx.enter_context(tc.tile_pool(name="keep", bufs=1))
-        banks = ctx.enter_context(tc.psum_pool(name="banks", bufs=4))
+        resident = ctx.enter_context(tc.tile_pool(name="resident", bufs=2 * PAIRS))
+        banks = ctx.enter_context(tc.psum_pool(name="banks", bufs=2 * RUN))
         proj_banks = ctx.enter_context(tc.psum_pool(name="proj_banks", bufs=3))
         score_banks = ctx.enter_context(tc.psum_pool(name="score_banks", bufs=1))
 
         x_rows = consts.tile([P, MODEL], BF16)
         nc.sync.dma_start(out=x_rows[:], in_=x.flatten_outer_dims())
         w_rows = []
-        for b in range(BLOCKS):
-            block_rows = rows_pool.tile([P, MODEL], BF16)
-            nc.sync.dma_start(out=block_rows[:], in_=Wqk[b * P : (b + 1) * P, :])
-            w_rows.append(block_rows)
+        for step in range(STEPS):
+            for i in range(RUN):
+                first_row = (step % 2) * HEADS * HEAD_DIM + ((step // 2) * RUN + i) * P
+                pair_rows = resident.tile([P, MODEL], BF16)
+                nc.sync.dma_start(out=pair_rows[:], in_=Wqk[first_row : first_row + P, :])
+                w_rows.append(pair_rows)
 
-        zero_values = consts.tile([P, BANK * PACK], BF16, align_bytes=64)
-        zero_codes = consts.tile([P, BANK], U32, align_bytes=64)
-        zero_scales = consts.tile([P, BANK], U8, align_bytes=64)
-        nc.vector.memset(zero_values[:].bitcast(I32), 0)
-        nc.vector.quantize_mx(
-            out=zero_codes[:].bitcast(FP8X4), scales=zero_scales[:], in_=zero_values[:]
-        )
-        zero_bank = score_banks.tile([P, BANK], F32, tag="scores")
-        for n in range(WARM_PASSES):
-            nc.tensor.matmul_mx(
-                out=zero_bank[:],
-                lhsT=zero_codes[:, :P].bitcast(FP8X4),
-                lhsT_scale=zero_scales[:, :P],
-                rhs=zero_codes[:].bitcast(FP8X4),
-                rhs_scale=zero_scales[:],
-                start=True,
-                stop=True,
-            )
-
+        warm = consts.tile([P, 1], F32)
+        nc.vector.memset(warm[:], 0.0)
+        nc.scalar.activation(out=warm[:], in_=warm[:], func=ACT.Exp)
+        q_grouped = consts.tile([P, GROUPS, TOKEN_PASSES, GROUP, 2, COLS], BF16, align_bytes=64)
+        nc.vector.memset(q_grouped[:].rearrange("p a r i e n -> p (a r i e n)").bitcast(I32), 0)
+        k_grouped = consts.tile([P, TOKEN_PASSES, PAIRS, COLS], BF16, align_bytes=64)
         identity = consts.tile([P, P], F32)
         make_identity(nc, identity[:])
         token_order = consts.tile([P, P], F32)
@@ -92,126 +86,107 @@ def tile_slidingwindowattention_pa_s_kernel(tc, x, Wqk, out):
             out=token_order[:].rearrange("p (r w t) -> p r w t", r=TOKEN_PASSES, w=WINDOW_ROWS),
             in_=identity[:].rearrange("p (w r t) -> p r w t", w=WINDOW_ROWS, r=TOKEN_PASSES),
         )
-        warm = consts.tile([P, 1], F32)
-        nc.vector.memset(warm[:], 0.0)
-        nc.scalar.activation(out=warm[:], in_=warm[:], func=ACT.Exp)
-        own_pair = consts.tile([P, QUERY_GROUPS, PAIRS, WINDOW_ROWS], F32)
-        nc.vector.memset(own_pair[:], 0.0)
-        for a in range(QUERY_GROUPS):
-            for i in range(GROUP):
-                nc.vector.memset(own_pair[32 * i : 32 * i + 32, a, GROUP * a + i, :], 1.0)
-        q_grouped = keep.tile(
-            [P, QUERY_GROUPS, TOKEN_PASSES, GROUP, 2, COLS], BF16, align_bytes=64
-        )
-        nc.vector.memset(q_grouped[:], 0.0)
-        k_grouped = keep.tile([P, TOKEN_PASSES, PAIRS, COLS], BF16, align_bytes=64)
 
         x_flipped = flip_rows(nc, banks, x_rows, token_order)
-        x_grouped = keep.tile([P, PASSES, TOKENS, PACK], BF16, align_bytes=64)
-        nc.scalar.copy(
+        x_grouped = consts.tile([P, PASSES, TOKENS, PACK], BF16, align_bytes=64)
+        nc.vector.tensor_copy(
             out=x_grouped[:].bitcast(F32), in_=x_flipped[:].rearrange("p g u n -> p g n u")
         )
-        x_codes = keep.tile([P, PASSES, TOKENS], U32, align_bytes=64)
-        x_scales = keep.tile([P, PASSES, TOKENS], U8, align_bytes=64)
-        nc.vector.quantize_mx(
-            out=x_codes[:].rearrange("p g n -> p (g n)").bitcast(FP8X4),
-            scales=x_scales[:].rearrange("p g n -> p (g n)"),
-            in_=x_grouped[:].rearrange("p g n t -> p (g n t)"),
+        x_codes, x_scales = quantise(
+            nc, consts, "x", x_grouped[:].rearrange("p g n t -> p (g n t)"), PASSES * TOKENS
         )
 
         w_codes = []
         w_scales = []
+        q_codes = []
+        q_scales = []
 
-        def quantise_group(c):
-            for i in range(GROUP):
-                flipped = flip_rows(nc, banks, w_rows[GROUP * c + i], identity)
-                grouped = packed.tile([P, PASSES, P, PACK], BF16, align_bytes=64)
-                copy = nc.vector.tensor_copy if i == 2 else nc.scalar.copy
-                copy(out=grouped[:].bitcast(F32), in_=flipped[:].rearrange("p g u m -> p g m u"))
-                codes = packed.tile([P, PASSES, P], U32, align_bytes=64)
-                scales = packed.tile([P, PASSES, P], U8, align_bytes=64)
-                nc.vector.quantize_mx(
-                    out=codes[:].rearrange("p g m -> p (g m)").bitcast(FP8X4),
-                    scales=scales[:].rearrange("p g m -> p (g m)"),
-                    in_=grouped[:].rearrange("p g m t -> p (g m t)"),
+        def quantise_step(step):
+            for i in range(RUN):
+                flipped = flip_rows(nc, banks, w_rows[step * RUN + i], identity)
+                grouped = resident.tile([P, PASSES, P, PACK], BF16, align_bytes=64)
+                nc.scalar.copy(
+                    out=grouped[:].bitcast(F32), in_=flipped[:].rearrange("p g u m -> p g m u")
+                )
+                codes, scales = quantise(
+                    nc, resident, "w", grouped[:].rearrange("p g m t -> p (g m t)"), PASSES * P
                 )
                 w_codes.append(codes)
                 w_scales.append(scales)
 
-        def project_group(c):
-            proj = proj_banks.tile([P, GROUP, TOKEN_PASSES, COLS], F32)
-            for i in range(GROUP):
-                b = GROUP * c + i
+        def project_step(step):
+            proj = proj_banks.tile([P, RUN, TOKEN_PASSES, COLS], F32)
+            for i in range(RUN):
                 for g in range(PASSES):
+                    span = slice(g * P, (g + 1) * P)
                     nc.tensor.matmul_mx(
                         out=proj[:, i, :, :].rearrange("p r n -> p (r n)"),
-                        lhsT=w_codes[b][:, g, :].bitcast(FP8X4),
-                        lhsT_scale=w_scales[b][:, g, :],
-                        rhs=x_codes[:, g, :].bitcast(FP8X4),
-                        rhs_scale=x_scales[:, g, :],
+                        lhsT=w_codes[step * RUN + i][:, span].bitcast(FP8X4),
+                        lhsT_scale=w_scales[step * RUN + i][:, span],
+                        rhs=x_codes[:, span].bitcast(FP8X4),
+                        rhs_scale=x_scales[:, span],
                         start=(g == 0),
                         stop=(g == PASSES - 1),
                     )
             by_pass = proj[:].rearrange("p i r n -> p r i n")
-            if c < QUERY_GROUPS:
+            first_pair = (step // 2) * RUN
+            if step % 2 == 0:
+                a = first_pair // GROUP
+                first = first_pair % GROUP
                 for e in range(2):
                     head = slice(HEAD_DIM * e, HEAD_DIM * (e + 1))
-                    nc.scalar.activation(
-                        out=q_grouped[head, c, :, :, e, :],
-                        in_=by_pass[head],
-                        func=ACT.Copy,
-                        scale=HEAD_DIM**-0.5,
+                    nc.vector.tensor_scalar_mul(
+                        out=q_grouped[head, a, :, first : first + RUN, e, :],
+                        in0=by_pass[head],
+                        scalar1=HEAD_DIM**-0.5,
                     )
+                if first + RUN == GROUP:
+                    codes, scales = quantise(
+                        nc,
+                        resident,
+                        "q",
+                        q_grouped[:, a].rearrange("p r i e n -> p (r i e n)"),
+                        TOKEN_PASSES * P,
+                    )
+                    q_codes.append(codes)
+                    q_scales.append(scales)
             else:
-                first = GROUP * (c - QUERY_GROUPS)
-                nc.vector.tensor_copy(out=k_grouped[:, :, first : first + GROUP, :], in_=by_pass)
+                nc.scalar.copy(out=k_grouped[:, :, first_pair : first_pair + RUN, :], in_=by_pass)
 
-        quantise_group(0)
-        for c in range(GROUPS):
-            if c + 1 < GROUPS:
-                quantise_group(c + 1)
-            project_group(c)
+        quantise_step(0)
+        for step in range(STEPS):
+            if step + 1 < STEPS:
+                quantise_step(step + 1)
+            project_step(step)
 
-        q_codes = keep.tile([P, QUERY_GROUPS, TOKEN_PASSES, P], U32, align_bytes=64)
-        q_scales = keep.tile([P, QUERY_GROUPS, TOKEN_PASSES, P], U8, align_bytes=64)
-        nc.vector.quantize_mx(
-            out=q_codes[:].rearrange("p a r m -> p (a r m)").bitcast(FP8X4),
-            scales=q_scales[:].rearrange("p a r m -> p (a r m)"),
-            in_=q_grouped[:].rearrange("p a r i e n -> p (a r i e n)"),
-        )
-        k_codes = keep.tile([P, TOKEN_PASSES, P], U32, align_bytes=64)
-        k_scales = keep.tile([P, TOKEN_PASSES, P], U8, align_bytes=64)
-        nc.vector.quantize_mx(
-            out=k_codes[:].rearrange("p r n -> p (r n)").bitcast(FP8X4),
-            scales=k_scales[:].rearrange("p r n -> p (r n)"),
-            in_=k_grouped[:].rearrange("p r c n -> p (r c n)"),
+        k_codes, k_scales = quantise(
+            nc, consts, "k", k_grouped[:].rearrange("p r c n -> p (r c n)"), TOKEN_PASSES * P
         )
 
-        all_pairs = score_banks.tile([P, QUERY_GROUPS, PAIRS, WINDOW_ROWS], F32, tag="scores")
-        for a in range(QUERY_GROUPS):
+        all_pairs = score_banks.tile([P, GROUPS * PAIRS, WINDOW_ROWS], F32)
+        for a in range(GROUPS):
             for r in range(TOKEN_PASSES):
+                span = slice(r * P, (r + 1) * P)
                 nc.tensor.matmul_mx(
-                    out=all_pairs[:, a, :, :].rearrange("p c v -> p (c v)"),
-                    lhsT=q_codes[:, a, r, :].bitcast(FP8X4),
-                    lhsT_scale=q_scales[:, a, r, :],
-                    rhs=k_codes[:, r, :].bitcast(FP8X4),
-                    rhs_scale=k_scales[:, r, :],
+                    out=all_pairs[:, a * PAIRS : (a + 1) * PAIRS, :].rearrange("p c v -> p (c v)"),
+                    lhsT=q_codes[a][:, span].bitcast(FP8X4),
+                    lhsT_scale=q_scales[a][:, span],
+                    rhs=k_codes[:, span].bitcast(FP8X4),
+                    rhs_scale=k_scales[:, span],
                     start=(r == 0),
                     stop=(r == TOKEN_PASSES - 1),
                 )
 
-        picked = keep.tile([P, QUERY_GROUPS, PAIRS, WINDOW_ROWS], F32)
-        nc.vector.tensor_tensor(out=picked[:], in0=all_pairs[:], in1=own_pair[:], op=ALU.mult)
-        scores = keep.tile([P, QUERY_GROUPS, WINDOW_ROWS], F32)
-        nc.vector.tensor_reduce(
-            out=scores[:], in_=picked[:].rearrange("p a c v -> p a v c"), axis=AXIS_X, op=ALU.add
-        )
+        scores = consts.tile([P, GROUPS, WINDOW_ROWS], F32)
+        for i in range(GROUP):
+            rows = slice(QUADRANT * i, QUADRANT * (i + 1))
+            nc.vector.tensor_copy(out=scores[rows], in_=all_pairs[rows, i :: PAIRS + GROUP, :])
 
-        neg_max = keep.tile([P, QUERY_GROUPS], F32)
+        neg_max = consts.tile([P, GROUPS], F32)
         nc.vector.tensor_reduce(out=neg_max[:], in_=scores[:], axis=AXIS_X, op=ALU.max, negate=True)
-        weights = keep.tile([P, QUERY_GROUPS, WINDOW_ROWS], F32)
-        row_sum = keep.tile([P, QUERY_GROUPS], F32)
-        for a in range(QUERY_GROUPS):
+        weights = consts.tile([P, GROUPS, WINDOW_ROWS], F32)
+        row_sum = consts.tile([P, GROUPS], F32)
+        for a in range(GROUPS):
             nc.scalar.activation(
                 out=weights[:, a, :],
                 in_=scores[:, a, :],
@@ -219,14 +194,12 @@ def tile_slidingwindowattention_pa_s_kernel(tc, x, Wqk, out):
                 bias=neg_max[:, a : a + 1],
                 accum_out=row_sum[:, a : a + 1],
             )
-        inverse = keep.tile([P, QUERY_GROUPS], F32)
+        inverse = consts.tile([P, GROUPS], F32)
         nc.vector.reciprocal(out=inverse[:], in_=row_sum[:])
         nc.vector.tensor_tensor(
             out=weights[:],
             in0=weights[:],
-            in1=inverse[:].unsqueeze(2).to_broadcast([P, QUERY_GROUPS, WINDOW_ROWS]),
+            in1=inverse[:].unsqueeze(2).to_broadcast([P, GROUPS, WINDOW_ROWS]),
             op=ALU.mult,
         )
-        nc.sync.dma_start(
-            out=out.rearrange("(a h) w v -> (h w) a v", a=QUERY_GROUPS), in_=weights[:]
-        )
+        nc.sync.dma_start(out=out.rearrange("(a h) w v -> (h w) a v", a=GROUPS), in_=weights[:])

@@ -30,8 +30,12 @@ COLS = WINDOW_ROWS * PACK
 QUADRANT = 32
 GROUP = P // QUADRANT
 GROUPS = PAIRS // GROUP
+OWN = GROUP * WINDOW_ROWS
 RUN = 2
-STEPS = 2 * PAIRS // RUN
+TILES = 2 * PAIRS
+RUNS = TILES // RUN
+GROUP_RUNS = GROUP // RUN
+AHEAD = 2
 
 FLOPS = 2 * TOKENS * MODEL * 2 * MODEL + HEADS * 2 * WINDOW_ROWS * WINDOW_ROWS * ROW_TOKENS * HEAD_DIM
 
@@ -58,27 +62,26 @@ def tile_slidingwindowattention_pa_s_kernel(tc, x, Wqk, out):
     with ExitStack() as ctx:
         ctx.enter_context(tc.manual_schedule())
         consts = ctx.enter_context(tc.tile_pool(name="consts", bufs=1))
-        resident = ctx.enter_context(tc.tile_pool(name="resident", bufs=2 * PAIRS))
-        banks = ctx.enter_context(tc.psum_pool(name="banks", bufs=2 * RUN))
-        proj_banks = ctx.enter_context(tc.psum_pool(name="proj_banks", bufs=3))
-        score_banks = ctx.enter_context(tc.psum_pool(name="score_banks", bufs=1))
+        resident = ctx.enter_context(tc.tile_pool(name="resident", bufs=TILES))
+        per_group = ctx.enter_context(tc.tile_pool(name="per_group", bufs=GROUPS))
+        banks = ctx.enter_context(tc.psum_pool(name="banks", bufs=4))
+        proj_banks = ctx.enter_context(tc.psum_pool(name="proj_banks", bufs=2))
+        score_banks = ctx.enter_context(tc.psum_pool(name="score_banks", bufs=GROUPS))
 
         x_rows = consts.tile([P, MODEL], BF16)
         nc.sync.dma_start(out=x_rows[:], in_=x.flatten_outer_dims())
         w_rows = []
-        for step in range(STEPS):
-            for i in range(RUN):
-                first_row = (step % 2) * HEADS * HEAD_DIM + ((step // 2) * RUN + i) * P
-                pair_rows = resident.tile([P, MODEL], BF16)
-                nc.sync.dma_start(out=pair_rows[:], in_=Wqk[first_row : first_row + P, :])
-                w_rows.append(pair_rows)
+        for j in range(TILES):
+            a, rest = divmod(j, 2 * GROUP)
+            is_key, i = divmod(rest, GROUP)
+            first_row = is_key * HEADS * HEAD_DIM + (a * GROUP + i) * P
+            pair_rows = resident.tile([P, MODEL], BF16)
+            nc.sync.dma_start(out=pair_rows[:], in_=Wqk[first_row : first_row + P, :])
+            w_rows.append(pair_rows)
 
         warm = consts.tile([P, 1], F32)
         nc.vector.memset(warm[:], 0.0)
         nc.scalar.activation(out=warm[:], in_=warm[:], func=ACT.Exp)
-        q_grouped = consts.tile([P, GROUPS, TOKEN_PASSES, GROUP, 2, COLS], BF16, align_bytes=64)
-        nc.vector.memset(q_grouped[:].rearrange("p a r i e n -> p (a r i e n)").bitcast(I32), 0)
-        k_grouped = consts.tile([P, TOKEN_PASSES, PAIRS, COLS], BF16, align_bytes=64)
         identity = consts.tile([P, P], F32)
         make_identity(nc, identity[:])
         token_order = consts.tile([P, P], F32)
@@ -87,100 +90,152 @@ def tile_slidingwindowattention_pa_s_kernel(tc, x, Wqk, out):
             in_=identity[:].rearrange("p (w r t) -> p r w t", w=WINDOW_ROWS, r=TOKEN_PASSES),
         )
 
+        q_codes = []
+        q_scales = []
+        k_codes = []
+        k_scales = []
+        q_values = []
+        k_values = []
+        for a in range(GROUPS):
+            codes = per_group.tile([P, TOKEN_PASSES * GROUP, 2, WINDOW_ROWS], U32, align_bytes=64, tag="qp_codes")
+            nc.gpsimd.memset(codes[:].rearrange("p c e w -> p (c e w)").bitcast(I32), 0)
+            q_codes.append(codes)
+            scales = per_group.tile([P, TOKEN_PASSES * GROUP, 2, WINDOW_ROWS], U8, align_bytes=64, tag="qp_scales")
+            q_scales.append(scales)
+            codes = per_group.tile([P, (TOKEN_PASSES + 1) * OWN], U32, align_bytes=64, tag="k_codes")
+            scales = per_group.tile([P, (TOKEN_PASSES + 1) * OWN], U8, align_bytes=64, tag="k_scales")
+            nc.gpsimd.memset(codes[:, TOKEN_PASSES * OWN :].bitcast(I32), 0)
+            nc.gpsimd.memset(scales[:, TOKEN_PASSES * OWN :].bitcast(I32), 0)
+            k_codes.append(codes)
+            k_scales.append(scales)
+            values = per_group.tile([P, TOKEN_PASSES, GROUP, COLS], BF16, align_bytes=64, tag="q_values")
+            q_values.append(values)
+            values = per_group.tile([P, TOKEN_PASSES, GROUP, COLS], BF16, align_bytes=64, tag="k_values")
+            k_values.append(values)
+
         x_flipped = flip_rows(nc, banks, x_rows, token_order)
         x_grouped = consts.tile([P, PASSES, TOKENS, PACK], BF16, align_bytes=64)
-        nc.vector.tensor_copy(
+        nc.scalar.copy(
             out=x_grouped[:].bitcast(F32), in_=x_flipped[:].rearrange("p g u n -> p g n u")
         )
         x_codes, x_scales = quantise(
             nc, consts, "x", x_grouped[:].rearrange("p g n t -> p (g n t)"), PASSES * TOKENS
         )
 
+        w_flipped = []
+        w_grouped = []
         w_codes = []
         w_scales = []
-        q_codes = []
-        q_scales = []
 
-        def quantise_step(step):
-            for i in range(RUN):
-                flipped = flip_rows(nc, banks, w_rows[step * RUN + i], identity)
-                grouped = resident.tile([P, PASSES, P, PACK], BF16, align_bytes=64)
-                nc.scalar.copy(
-                    out=grouped[:].bitcast(F32), in_=flipped[:].rearrange("p g u m -> p g m u")
-                )
-                codes, scales = quantise(
-                    nc, resident, "w", grouped[:].rearrange("p g m t -> p (g m t)"), PASSES * P
-                )
-                w_codes.append(codes)
-                w_scales.append(scales)
+        def regroup(j):
+            grouped = resident.tile([P, PASSES, P, PACK], BF16, align_bytes=64)
+            copy = nc.vector.tensor_copy if j % 3 == 1 else nc.scalar.copy
+            copy(out=grouped[:].bitcast(F32), in_=w_flipped[j][:].rearrange("p g u m -> p g m u"))
+            w_grouped.append(grouped)
 
-        def project_step(step):
+        def quantise_tile(j):
+            codes, scales = quantise(
+                nc, resident, "w", w_grouped[j][:].rearrange("p g m t -> p (g m t)"), PASSES * P
+            )
+            w_codes.append(codes)
+            w_scales.append(scales)
+
+        def project(run):
             proj = proj_banks.tile([P, RUN, TOKEN_PASSES, COLS], F32)
             for i in range(RUN):
+                j = run * RUN + i
                 for g in range(PASSES):
                     span = slice(g * P, (g + 1) * P)
                     nc.tensor.matmul_mx(
                         out=proj[:, i, :, :].rearrange("p r n -> p (r n)"),
-                        lhsT=w_codes[step * RUN + i][:, span].bitcast(FP8X4),
-                        lhsT_scale=w_scales[step * RUN + i][:, span],
+                        lhsT=w_codes[j][:, span].bitcast(FP8X4),
+                        lhsT_scale=w_scales[j][:, span],
                         rhs=x_codes[:, span].bitcast(FP8X4),
                         rhs_scale=x_scales[:, span],
                         start=(g == 0),
                         stop=(g == PASSES - 1),
                     )
             by_pass = proj[:].rearrange("p i r n -> p r i n")
-            first_pair = (step // 2) * RUN
-            if step % 2 == 0:
-                a = first_pair // GROUP
-                first = first_pair % GROUP
-                for e in range(2):
-                    head = slice(HEAD_DIM * e, HEAD_DIM * (e + 1))
-                    nc.vector.tensor_scalar_mul(
-                        out=q_grouped[head, a, :, first : first + RUN, e, :],
-                        in0=by_pass[head],
-                        scalar1=HEAD_DIM**-0.5,
-                    )
-                if first + RUN == GROUP:
-                    codes, scales = quantise(
-                        nc,
-                        resident,
-                        "q",
-                        q_grouped[:, a].rearrange("p r i e n -> p (r i e n)"),
-                        TOKEN_PASSES * P,
-                    )
-                    q_codes.append(codes)
-                    q_scales.append(scales)
+            a, rest = divmod(run, 2 * GROUP_RUNS)
+            is_key, part = divmod(rest, GROUP_RUNS)
+            pairs = slice(part * RUN, (part + 1) * RUN)
+            if is_key:
+                nc.scalar.copy(out=k_values[a][:, :, pairs, :], in_=by_pass)
             else:
-                nc.scalar.copy(out=k_grouped[:, :, first_pair : first_pair + RUN, :], in_=by_pass)
+                nc.scalar.mul(q_values[a][:, :, pairs, :], by_pass, HEAD_DIM**-0.5)
 
-        quantise_step(0)
-        for step in range(STEPS):
-            if step + 1 < STEPS:
-                quantise_step(step + 1)
-            project_step(step)
+        def quantise_queries(a):
+            codes, scales = quantise(
+                nc, per_group, "q", q_values[a][:].rearrange("p r i n -> p (r i n)"), TOKEN_PASSES * OWN
+            )
+            for e in range(2):
+                head = slice(HEAD_DIM * e, HEAD_DIM * (e + 1))
+                nc.vector.tensor_copy(
+                    out=q_codes[a][head, :, e, :].bitcast(I32),
+                    in_=codes[head].rearrange("p (c w) -> p c w", w=WINDOW_ROWS).bitcast(I32),
+                )
+                nc.vector.tensor_copy(
+                    out=q_scales[a][:, :, e, :],
+                    in_=scales[:].rearrange("p (c w) -> p c w", w=WINDOW_ROWS),
+                )
 
-        k_codes, k_scales = quantise(
-            nc, consts, "k", k_grouped[:].rearrange("p r c n -> p (r c n)"), TOKEN_PASSES * P
-        )
+        def quantise_keys(a):
+            nc.vector.quantize_mx(
+                out=k_codes[a][:, : TOKEN_PASSES * OWN].bitcast(FP8X4),
+                scales=k_scales[a][:, : TOKEN_PASSES * OWN],
+                in_=k_values[a][:].rearrange("p r i n -> p (r i n)"),
+            )
 
-        all_pairs = score_banks.tile([P, GROUPS * PAIRS, WINDOW_ROWS], F32)
-        for a in range(GROUPS):
+        scores = consts.tile([P, GROUPS, WINDOW_ROWS], F32)
+        score_tiles = []
+
+        def score_passes(a):
+            group_scores = score_banks.tile([P, 2 * OWN], F32)
             for r in range(TOKEN_PASSES):
-                span = slice(r * P, (r + 1) * P)
+                span = slice(r * OWN, (r + 2) * OWN)
+                rows = slice(r * GROUP, (r + 1) * GROUP)
                 nc.tensor.matmul_mx(
-                    out=all_pairs[:, a * PAIRS : (a + 1) * PAIRS, :].rearrange("p c v -> p (c v)"),
-                    lhsT=q_codes[a][:, span].bitcast(FP8X4),
-                    lhsT_scale=q_scales[a][:, span],
-                    rhs=k_codes[:, span].bitcast(FP8X4),
-                    rhs_scale=k_scales[:, span],
+                    out=group_scores[:],
+                    lhsT=q_codes[a][:, rows].rearrange("p c e w -> p (c e w)").bitcast(FP8X4),
+                    lhsT_scale=q_scales[a][:, rows].rearrange("p c e w -> p (c e w)"),
+                    rhs=k_codes[a][:, span].bitcast(FP8X4),
+                    rhs_scale=k_scales[a][:, span],
                     start=(r == 0),
                     stop=(r == TOKEN_PASSES - 1),
                 )
+            score_tiles.append(group_scores)
 
-        scores = consts.tile([P, GROUPS, WINDOW_ROWS], F32)
-        for i in range(GROUP):
-            rows = slice(QUADRANT * i, QUADRANT * (i + 1))
-            nc.vector.tensor_copy(out=scores[rows], in_=all_pairs[rows, i :: PAIRS + GROUP, :])
+        def pick_own(a):
+            for i in range(GROUP):
+                rows = slice(QUADRANT * i, QUADRANT * (i + 1))
+                cols = slice(WINDOW_ROWS * i, WINDOW_ROWS * (i + 1))
+                nc.vector.tensor_copy(out=scores[rows, a, :], in_=score_tiles[a][rows, cols])
+
+        for step in range(RUNS + AHEAD):
+            tiles = range(step * RUN, (step + 1) * RUN) if step < RUNS else []
+            for j in tiles:
+                w_flipped.append(flip_rows(nc, banks, w_rows[j], identity))
+            for j in tiles:
+                regroup(j)
+                if j > 0:
+                    quantise_tile(j - 1)
+            if step == RUNS:
+                quantise_tile(TILES - 1)
+            for a in range(GROUPS):
+                if step == AHEAD + 2 * GROUP_RUNS * a + GROUP_RUNS:
+                    quantise_queries(a)
+            if step == AHEAD + 2 * GROUP_RUNS:
+                quantise_keys(0)
+            if step >= AHEAD:
+                project(step - AHEAD)
+            if step == AHEAD + 2 * GROUP_RUNS + 1:
+                score_passes(0)
+            if step == AHEAD + 2 * GROUP_RUNS + 2:
+                pick_own(0)
+
+        quantise_keys(1)
+        score_passes(1)
+        pick_own(1)
 
         neg_max = consts.tile([P, GROUPS], F32)
         nc.vector.tensor_reduce(out=neg_max[:], in_=scores[:], axis=AXIS_X, op=ALU.max, negate=True)

@@ -37,6 +37,8 @@ RUNS = TILES // RUN
 GROUP_RUNS = GROUP // RUN
 AHEAD = 2
 
+WARM_UPS = 5
+
 FLOPS = 2 * TOKENS * MODEL * 2 * MODEL + HEADS * 2 * WINDOW_ROWS * WINDOW_ROWS * ROW_TOKENS * HEAD_DIM
 
 
@@ -82,6 +84,11 @@ def tile_slidingwindowattention_pa_s_kernel(tc, x, Wqk, out):
         warm = consts.tile([P, 1], F32)
         nc.vector.memset(warm[:], 0.0)
         nc.scalar.activation(out=warm[:], in_=warm[:], func=ACT.Exp)
+        zeros = consts.tile([P, P], F32)
+        nc.vector.memset(zeros[:], 0.0)
+        unread = proj_banks.tile([P, P], F32, tag="proj")
+        for i in range(WARM_UPS):
+            nc.tensor.matmul(out=unread[:], lhsT=zeros[:], rhs=zeros[:], start=True, stop=True)
         identity = consts.tile([P, P], F32)
         make_identity(nc, identity[:])
         token_order = consts.tile([P, P], F32)

@@ -43,7 +43,7 @@ FLOPS = 2 * TOKENS * MODEL * 2 * MODEL + HEADS * 2 * WINDOW_ROWS * WINDOW_ROWS *
 
 
 def flip_rows(nc, banks, rows, order):
-    words = rows[:].bitcast(F32)
+    words = rows.bitcast(F32)
     flipped = banks.tile([P, PASSES, HALVES, P], F32, tag="flipped")
     for g in range(PASSES):
         for u in range(HALVES):
@@ -73,13 +73,19 @@ def tile_slidingwindowattention_pa_s_kernel(tc, x, Wqk, out):
         x_rows = consts.tile([P, MODEL], BF16)
         nc.sync.dma_start(out=x_rows[:], in_=x.flatten_outer_dims())
         w_rows = []
-        for j in range(TILES):
-            a, rest = divmod(j, 2 * GROUP)
+        for run in range(RUNS):
+            a, rest = divmod(run * RUN, 2 * GROUP)
             is_key, i = divmod(rest, GROUP)
             first_row = is_key * HEADS * HEAD_DIM + (a * GROUP + i) * P
-            pair_rows = resident.tile([P, MODEL], BF16)
-            nc.sync.dma_start(out=pair_rows[:], in_=Wqk[first_row : first_row + P, :])
-            w_rows.append(pair_rows)
+            run_rows = resident.tile([P, RUN, MODEL], BF16)
+            source = Wqk[first_row : first_row + RUN * P, :].rearrange("(t p) k -> p t k", t=RUN)
+            if run in (0, RUNS - 1):
+                for t in range(RUN):
+                    nc.sync.dma_start(out=run_rows[:, t, :], in_=source[:, t, :])
+            else:
+                nc.sync.dma_start(out=run_rows[:], in_=source)
+            for t in range(RUN):
+                w_rows.append(run_rows[:, t, :])
 
         warm = consts.tile([P, 1], F32)
         nc.vector.memset(warm[:], 0.0)
@@ -120,7 +126,7 @@ def tile_slidingwindowattention_pa_s_kernel(tc, x, Wqk, out):
             values = per_group.tile([P, TOKEN_PASSES, GROUP, COLS], BF16, align_bytes=64, tag="k_values")
             k_values.append(values)
 
-        x_flipped = flip_rows(nc, banks, x_rows, token_order)
+        x_flipped = flip_rows(nc, banks, x_rows[:], token_order)
         x_grouped = consts.tile([P, PASSES, TOKENS, PACK], BF16, align_bytes=64)
         nc.scalar.copy(
             out=x_grouped[:].bitcast(F32), in_=x_flipped[:].rearrange("p g u n -> p g n u")

@@ -68,7 +68,7 @@ def tile_slidingwindowattention_pa_s_kernel(tc, x, Wqk, out):
         per_group = ctx.enter_context(tc.tile_pool(name="per_group", bufs=GROUPS))
         banks = ctx.enter_context(tc.psum_pool(name="banks", bufs=4))
         proj_banks = ctx.enter_context(tc.psum_pool(name="proj_banks", bufs=2))
-        score_banks = ctx.enter_context(tc.psum_pool(name="score_banks", bufs=GROUPS))
+        score_banks = ctx.enter_context(tc.psum_pool(name="score_banks", bufs=1))
 
         x_rows = consts.tile([P, MODEL], BF16)
         nc.sync.dma_start(out=x_rows[:], in_=x.flatten_outer_dims())
@@ -92,9 +92,24 @@ def tile_slidingwindowattention_pa_s_kernel(tc, x, Wqk, out):
         nc.scalar.activation(out=warm[:], in_=warm[:], func=ACT.Exp)
         zeros = consts.tile([P, P], F32)
         nc.vector.memset(zeros[:], 0.0)
-        unread = proj_banks.tile([P, P], F32, tag="proj")
+        unread = score_banks.tile([P, PASSES * TOKENS], F32)
+
+        def keep_clock_plain():
+            nc.tensor.matmul(out=unread[:, :P], lhsT=zeros[:], rhs=zeros[:], start=True, stop=True)
+
+        def keep_clock_mx(j):
+            nc.tensor.matmul_mx(
+                out=unread[:],
+                lhsT=w_codes[j][:, :P].bitcast(FP8X4),
+                lhsT_scale=w_scales[j][:, :P],
+                rhs=x_codes[:].bitcast(FP8X4),
+                rhs_scale=x_scales[:],
+                start=True,
+                stop=True,
+            )
+
         for i in range(WARM_UPS):
-            nc.tensor.matmul(out=unread[:], lhsT=zeros[:], rhs=zeros[:], start=True, stop=True)
+            keep_clock_plain()
         identity = consts.tile([P, P], F32)
         make_identity(nc, identity[:])
         token_order = consts.tile([P, P], F32)
@@ -127,6 +142,7 @@ def tile_slidingwindowattention_pa_s_kernel(tc, x, Wqk, out):
             k_values.append(values)
 
         x_flipped = flip_rows(nc, banks, x_rows[:], token_order)
+        keep_clock_plain()
         x_grouped = consts.tile([P, PASSES, TOKENS, PACK], BF16, align_bytes=64)
         nc.scalar.copy(
             out=x_grouped[:].bitcast(F32), in_=x_flipped[:].rearrange("p g u n -> p g n u")
@@ -200,15 +216,14 @@ def tile_slidingwindowattention_pa_s_kernel(tc, x, Wqk, out):
             )
 
         scores = consts.tile([P, GROUPS, WINDOW_ROWS], F32)
-        score_tiles = []
+        all_scores = score_banks.tile([P, GROUPS, 2 * OWN], F32)
 
         def score_passes(a):
-            group_scores = score_banks.tile([P, 2 * OWN], F32)
             for r in range(TOKEN_PASSES):
                 span = slice(r * OWN, (r + 2) * OWN)
                 rows = slice(r * GROUP, (r + 1) * GROUP)
                 nc.tensor.matmul_mx(
-                    out=group_scores[:],
+                    out=all_scores[:, a, :],
                     lhsT=q_codes[a][:, rows].rearrange("p c e w -> p (c e w)").bitcast(FP8X4),
                     lhsT_scale=q_scales[a][:, rows].rearrange("p c e w -> p (c e w)"),
                     rhs=k_codes[a][:, span].bitcast(FP8X4),
@@ -216,18 +231,19 @@ def tile_slidingwindowattention_pa_s_kernel(tc, x, Wqk, out):
                     start=(r == 0),
                     stop=(r == TOKEN_PASSES - 1),
                 )
-            score_tiles.append(group_scores)
 
         def pick_own(a):
             for i in range(GROUP):
                 rows = slice(QUADRANT * i, QUADRANT * (i + 1))
                 cols = slice(WINDOW_ROWS * i, WINDOW_ROWS * (i + 1))
-                nc.vector.tensor_copy(out=scores[rows, a, :], in_=score_tiles[a][rows, cols])
+                nc.vector.tensor_copy(out=scores[rows, a, :], in_=all_scores[rows, a, cols])
 
         for step in range(RUNS + AHEAD):
             tiles = range(step * RUN, (step + 1) * RUN) if step < RUNS else []
             for j in tiles:
                 w_flipped.append(flip_rows(nc, banks, w_rows[j], identity))
+            if step < AHEAD:
+                keep_clock_plain()
             for j in tiles:
                 regroup(j)
                 if j > 0:
@@ -241,6 +257,7 @@ def tile_slidingwindowattention_pa_s_kernel(tc, x, Wqk, out):
                 quantise_keys(0)
             if step >= AHEAD:
                 project(step - AHEAD)
+                keep_clock_mx((step - AHEAD) * RUN)
             if step == AHEAD + 2 * GROUP_RUNS + 1:
                 score_passes(0)
             if step == AHEAD + 2 * GROUP_RUNS + 2:

@@ -44,12 +44,13 @@ FLOPS = 2 * TOKENS * MODEL * 2 * MODEL + HEADS * 2 * WINDOW_ROWS * WINDOW_ROWS *
 
 def flip_rows(nc, banks, rows, order):
     words = rows.bitcast(F32)
-    flipped = banks.tile([P, PASSES, HALVES, P], F32, tag="flipped")
-    for g in range(PASSES):
+    passes = words.shape[1] // (HALVES * P)
+    flipped = banks.tile([P, passes, HALVES, P], F32, tag="flipped")
+    for g in range(passes):
         for u in range(HALVES):
             first = (g * HALVES + u) * P
             nc.tensor.transpose(flipped[:, g, u, :], words[:, first : first + P], order[:])
-    return flipped
+    return flipped[:]
 
 
 def quantise(nc, pool, name, grouped, columns):
@@ -74,14 +75,15 @@ def tile_slidingwindowattention_pa_s_kernel(tc, x, Wqk, out):
         nc.sync.dma_start(out=x_rows[:], in_=x.flatten_outer_dims())
         w_rows = []
         for run in range(RUNS):
-            a, rest = divmod(run * RUN, 2 * GROUP)
-            is_key, i = divmod(rest, GROUP)
-            first_row = is_key * HEADS * HEAD_DIM + (a * GROUP + i) * P
+            first_row = run * RUN * P
             run_rows = resident.tile([P, RUN, MODEL], BF16)
             source = Wqk[first_row : first_row + RUN * P, :].rearrange("(t p) k -> p t k", t=RUN)
             if run in (0, RUNS - 1):
                 for t in range(RUN):
-                    nc.sync.dma_start(out=run_rows[:, t, :], in_=source[:, t, :])
+                    parts = PASSES if run * RUN + t == TILES - 1 else 1
+                    for part in range(parts):
+                        cols = slice(part * MODEL // parts, (part + 1) * MODEL // parts)
+                        nc.sync.dma_start(out=run_rows[:, t, cols], in_=source[:, t, cols])
             else:
                 nc.sync.dma_start(out=run_rows[:], in_=source)
             for t in range(RUN):
@@ -92,16 +94,19 @@ def tile_slidingwindowattention_pa_s_kernel(tc, x, Wqk, out):
         nc.scalar.activation(out=warm[:], in_=warm[:], func=ACT.Exp)
         zeros = consts.tile([P, P], F32)
         nc.vector.memset(zeros[:], 0.0)
-        unread = score_banks.tile([P, PASSES * TOKENS], F32)
+        scores_0 = score_banks.tile([P, 2 * OWN], F32)
+        scores_1 = score_banks.tile([P, 512], F32)
+        group_scores = [scores_0[:], scores_1[:, : 2 * OWN]]
+        unread = scores_1[:, 2 * OWN : 2 * OWN + PASSES * TOKENS]
 
         def keep_clock_plain():
             nc.tensor.matmul(out=unread[:, :P], lhsT=zeros[:], rhs=zeros[:], start=True, stop=True)
 
         def keep_clock_mx(j):
             nc.tensor.matmul_mx(
-                out=unread[:],
-                lhsT=w_codes[j][:, :P].bitcast(FP8X4),
-                lhsT_scale=w_scales[j][:, :P],
+                out=unread,
+                lhsT=w_parts[j][0][0].bitcast(FP8X4),
+                lhsT_scale=w_parts[j][0][1],
                 rhs=x_codes[:].bitcast(FP8X4),
                 rhs_scale=x_scales[:],
                 start=True,
@@ -145,7 +150,7 @@ def tile_slidingwindowattention_pa_s_kernel(tc, x, Wqk, out):
         keep_clock_plain()
         x_grouped = consts.tile([P, PASSES, TOKENS, PACK], BF16, align_bytes=64)
         nc.scalar.copy(
-            out=x_grouped[:].bitcast(F32), in_=x_flipped[:].rearrange("p g u n -> p g n u")
+            out=x_grouped[:].bitcast(F32), in_=x_flipped.rearrange("p g u n -> p g n u")
         )
         x_codes, x_scales = quantise(
             nc, consts, "x", x_grouped[:].rearrange("p g n t -> p (g n t)"), PASSES * TOKENS
@@ -153,41 +158,40 @@ def tile_slidingwindowattention_pa_s_kernel(tc, x, Wqk, out):
 
         w_flipped = []
         w_grouped = []
-        w_codes = []
-        w_scales = []
+        w_parts = []
 
         def regroup(j):
             grouped = resident.tile([P, PASSES, P, PACK], BF16, align_bytes=64)
             copy = nc.vector.tensor_copy if j % 3 == 1 else nc.scalar.copy
-            copy(out=grouped[:].bitcast(F32), in_=w_flipped[j][:].rearrange("p g u m -> p g m u"))
+            copy(out=grouped[:].bitcast(F32), in_=w_flipped[j].rearrange("p g u m -> p g m u"))
             w_grouped.append(grouped)
 
         def quantise_tile(j):
             codes, scales = quantise(
                 nc, resident, "w", w_grouped[j][:].rearrange("p g m t -> p (g m t)"), PASSES * P
             )
-            w_codes.append(codes)
-            w_scales.append(scales)
+            w_parts.append(
+                [(codes[:, g * P : (g + 1) * P], scales[:, g * P : (g + 1) * P]) for g in range(PASSES)]
+            )
 
-        def project(run):
+        def project(tiles):
             proj = proj_banks.tile([P, RUN, TOKEN_PASSES, COLS], F32)
-            for i in range(RUN):
-                j = run * RUN + i
+            for i, j in enumerate(tiles):
                 for g in range(PASSES):
-                    span = slice(g * P, (g + 1) * P)
+                    codes, scales = w_parts[j][g]
                     nc.tensor.matmul_mx(
                         out=proj[:, i, :, :].rearrange("p r n -> p (r n)"),
-                        lhsT=w_codes[j][:, span].bitcast(FP8X4),
-                        lhsT_scale=w_scales[j][:, span],
-                        rhs=x_codes[:, span].bitcast(FP8X4),
-                        rhs_scale=x_scales[:, span],
+                        lhsT=codes.bitcast(FP8X4),
+                        lhsT_scale=scales,
+                        rhs=x_codes[:, g * P : (g + 1) * P].bitcast(FP8X4),
+                        rhs_scale=x_scales[:, g * P : (g + 1) * P],
                         start=(g == 0),
                         stop=(g == PASSES - 1),
                     )
-            by_pass = proj[:].rearrange("p i r n -> p r i n")
-            a, rest = divmod(run, 2 * GROUP_RUNS)
-            is_key, part = divmod(rest, GROUP_RUNS)
-            pairs = slice(part * RUN, (part + 1) * RUN)
+            by_pass = proj[:, : len(tiles)].rearrange("p i r n -> p r i n")
+            is_key, pair = divmod(tiles[0], PAIRS)
+            a, first = divmod(pair, GROUP)
+            pairs = slice(first, first + len(tiles))
             if is_key:
                 nc.scalar.copy(out=k_values[a][:, :, pairs, :], in_=by_pass)
             else:
@@ -215,15 +219,14 @@ def tile_slidingwindowattention_pa_s_kernel(tc, x, Wqk, out):
                 in_=k_values[a][:].rearrange("p r i n -> p (r i n)"),
             )
 
-        scores = consts.tile([P, GROUPS, WINDOW_ROWS], F32)
-        all_scores = score_banks.tile([P, GROUPS, 2 * OWN], F32)
+        scores = consts.tile([P, 1, WINDOW_ROWS], F32)
 
         def score_passes(a):
             for r in range(TOKEN_PASSES):
                 span = slice(r * OWN, (r + 2) * OWN)
                 rows = slice(r * GROUP, (r + 1) * GROUP)
                 nc.tensor.matmul_mx(
-                    out=all_scores[:, a, :],
+                    out=group_scores[a],
                     lhsT=q_codes[a][:, rows].rearrange("p c e w -> p (c e w)").bitcast(FP8X4),
                     lhsT_scale=q_scales[a][:, rows].rearrange("p c e w -> p (c e w)"),
                     rhs=k_codes[a][:, span].bitcast(FP8X4),
@@ -236,10 +239,18 @@ def tile_slidingwindowattention_pa_s_kernel(tc, x, Wqk, out):
             for i in range(GROUP):
                 rows = slice(QUADRANT * i, QUADRANT * (i + 1))
                 cols = slice(WINDOW_ROWS * i, WINDOW_ROWS * (i + 1))
-                nc.vector.tensor_copy(out=scores[rows, a, :], in_=all_scores[rows, a, cols])
+                nc.vector.tensor_copy(out=scores[rows, a, :], in_=group_scores[a][rows, cols])
 
-        for step in range(RUNS + AHEAD):
-            tiles = range(step * RUN, (step + 1) * RUN) if step < RUNS else []
+        def normalise_and_store(exps, row_sum, a):
+            inverse = per_group.tile([P, 1], F32, tag="inverse")
+            nc.vector.reciprocal(out=inverse[:], in_=row_sum[:])
+            weights = per_group.tile([P, WINDOW_ROWS], F32, tag="weights")
+            nc.vector.tensor_scalar_mul(out=weights[:], in0=exps[:], scalar1=inverse[:])
+            nc.sync.dma_start(out=out.flatten_outer_dims()[a * P : (a + 1) * P, :], in_=weights[:])
+
+        LAST = TILES - 1
+        for step in range(RUNS - 1):
+            tiles = range(step * RUN, (step + 1) * RUN)
             for j in tiles:
                 w_flipped.append(flip_rows(nc, banks, w_rows[j], identity))
             if step < AHEAD:
@@ -248,43 +259,69 @@ def tile_slidingwindowattention_pa_s_kernel(tc, x, Wqk, out):
                 regroup(j)
                 if j > 0:
                     quantise_tile(j - 1)
-            if step == RUNS:
-                quantise_tile(TILES - 1)
             for a in range(GROUPS):
-                if step == AHEAD + 2 * GROUP_RUNS * a + GROUP_RUNS:
+                if step == AHEAD + GROUP_RUNS * (a + 1):
                     quantise_queries(a)
-            if step == AHEAD + 2 * GROUP_RUNS:
-                quantise_keys(0)
             if step >= AHEAD:
-                project(step - AHEAD)
-                keep_clock_mx((step - AHEAD) * RUN)
-            if step == AHEAD + 2 * GROUP_RUNS + 1:
-                score_passes(0)
-            if step == AHEAD + 2 * GROUP_RUNS + 2:
-                pick_own(0)
+                first = (step - AHEAD) * RUN
+                project([first, first + 1])
+                keep_clock_mx(first)
 
+        project([LAST - 5, LAST - 4])
+        w_flipped.append(flip_rows(nc, banks, w_rows[LAST - 1], identity))
+        halves = []
+        for g in range(PASSES):
+            cols = slice(g * MODEL // PASSES, (g + 1) * MODEL // PASSES)
+            halves.append(flip_rows(nc, banks, w_rows[LAST][:, cols], identity))
+        quantise_tile(LAST - 2)
+        quantise_keys(0)
+        regroup(LAST - 1)
+        half_grouped = []
+        for g in range(PASSES):
+            grouped = per_group.tile([P, P, PACK], BF16, align_bytes=64, tag="half_grouped")
+            copy = nc.vector.tensor_copy if g == 1 else nc.scalar.copy
+            copy(out=grouped[:].bitcast(F32), in_=halves[g].rearrange("p o u m -> p (o m) u"))
+            half_grouped.append(grouped)
+        project([LAST - 3, LAST - 2])
+        score_passes(0)
+        quantise_tile(LAST - 1)
+        parts = []
+        for g in range(PASSES):
+            codes, scales = quantise(
+                nc, per_group, "half", half_grouped[g][:].rearrange("p m t -> p (m t)"), P
+            )
+            parts.append((codes[:], scales[:]))
+        w_parts.append(parts)
+        project([LAST - 1])
+        project([LAST])
+
+        pick_own(0)
+        neg_max = per_group.tile([P, 1], F32, tag="neg_max")
+        nc.vector.tensor_reduce(out=neg_max[:], in_=scores[:, 0, :], axis=AXIS_X, op=ALU.max, negate=True)
+        exps = per_group.tile([P, WINDOW_ROWS], F32, tag="exps")
+        row_sum = per_group.tile([P, 1], F32, tag="row_sum")
+        nc.scalar.activation(out=exps[:], in_=scores[:, 0, :], func=ACT.Exp, bias=neg_max[:], accum_out=row_sum[:])
         quantise_keys(1)
         score_passes(1)
-        pick_own(1)
+        normalise_and_store(exps, row_sum, 0)
 
-        neg_max = consts.tile([P, GROUPS], F32)
-        nc.vector.tensor_reduce(out=neg_max[:], in_=scores[:], axis=AXIS_X, op=ALU.max, negate=True)
-        weights = consts.tile([P, GROUPS, WINDOW_ROWS], F32)
-        row_sum = consts.tile([P, GROUPS], F32)
-        for a in range(GROUPS):
-            nc.scalar.activation(
-                out=weights[:, a, :],
-                in_=scores[:, a, :],
-                func=ACT.Exp,
-                bias=neg_max[:, a : a + 1],
-                accum_out=row_sum[:, a : a + 1],
+        neg_max = per_group.tile([P, 1], F32, tag="neg_max")
+        exps = per_group.tile([P, WINDOW_ROWS], F32, tag="exps")
+        row_sum = per_group.tile([P, 1], F32, tag="row_sum")
+        for i in range(GROUP):
+            rows = slice(QUADRANT * i, QUADRANT * (i + 1))
+            cols = slice(WINDOW_ROWS * i, WINDOW_ROWS * (i + 1))
+            nc.vector.tensor_reduce(
+                out=neg_max[rows], in_=group_scores[1][rows, cols], axis=AXIS_X, op=ALU.max, negate=True
             )
-        inverse = consts.tile([P, GROUPS], F32)
-        nc.vector.reciprocal(out=inverse[:], in_=row_sum[:])
-        nc.vector.tensor_tensor(
-            out=weights[:],
-            in0=weights[:],
-            in1=inverse[:].unsqueeze(2).to_broadcast([P, GROUPS, WINDOW_ROWS]),
-            op=ALU.mult,
-        )
-        nc.sync.dma_start(out=out.rearrange("(a h) w v -> (h w) a v", a=GROUPS), in_=weights[:])
+        for i in range(GROUP):
+            rows = slice(QUADRANT * i, QUADRANT * (i + 1))
+            cols = slice(WINDOW_ROWS * i, WINDOW_ROWS * (i + 1))
+            nc.scalar.activation(
+                out=exps[rows],
+                in_=group_scores[1][rows, cols],
+                func=ACT.Exp,
+                bias=neg_max[rows],
+                accum_out=row_sum[rows],
+            )
+        normalise_and_store(exps, row_sum, 1)

@@ -78,7 +78,7 @@ def tile_slidingwindowattention_pa_s_kernel(tc, x, Wqk, out):
             first_row = run * RUN * P
             run_rows = resident.tile([P, RUN, MODEL], BF16)
             source = Wqk[first_row : first_row + RUN * P, :].rearrange("(t p) k -> p t k", t=RUN)
-            if run in (0, RUNS - 1):
+            if run in (0, RUNS - 2, RUNS - 1):
                 for t in range(RUN):
                     parts = PASSES if run * RUN + t == TILES - 1 else 1
                     for part in range(parts):
@@ -162,7 +162,7 @@ def tile_slidingwindowattention_pa_s_kernel(tc, x, Wqk, out):
 
         def regroup(j):
             grouped = resident.tile([P, PASSES, P, PACK], BF16, align_bytes=64)
-            copy = nc.vector.tensor_copy if j % 3 == 1 else nc.scalar.copy
+            copy = nc.vector.tensor_copy if j in (1, 4, 7) else nc.scalar.copy
             copy(out=grouped[:].bitcast(F32), in_=w_flipped[j].rearrange("p g u m -> p g m u"))
             w_grouped.append(grouped)
 
@@ -259,9 +259,8 @@ def tile_slidingwindowattention_pa_s_kernel(tc, x, Wqk, out):
                 regroup(j)
                 if j > 0:
                     quantise_tile(j - 1)
-            for a in range(GROUPS):
-                if step == AHEAD + GROUP_RUNS * (a + 1):
-                    quantise_queries(a)
+            if step == AHEAD + GROUP_RUNS:
+                quantise_queries(0)
             if step >= AHEAD:
                 first = (step - AHEAD) * RUN
                 project([first, first + 1])
@@ -283,7 +282,6 @@ def tile_slidingwindowattention_pa_s_kernel(tc, x, Wqk, out):
             copy(out=grouped[:].bitcast(F32), in_=halves[g].rearrange("p o u m -> p (o m) u"))
             half_grouped.append(grouped)
         project([LAST - 3, LAST - 2])
-        score_passes(0)
         quantise_tile(LAST - 1)
         parts = []
         for g in range(PASSES):
@@ -294,6 +292,10 @@ def tile_slidingwindowattention_pa_s_kernel(tc, x, Wqk, out):
         w_parts.append(parts)
         project([LAST - 1])
         project([LAST])
+        quantise_queries(1)
+        score_passes(0)
+        quantise_keys(1)
+        score_passes(1)
 
         pick_own(0)
         neg_max = per_group.tile([P, 1], F32, tag="neg_max")
@@ -301,10 +303,8 @@ def tile_slidingwindowattention_pa_s_kernel(tc, x, Wqk, out):
         exps = per_group.tile([P, WINDOW_ROWS], F32, tag="exps")
         row_sum = per_group.tile([P, 1], F32, tag="row_sum")
         nc.scalar.activation(out=exps[:], in_=scores[:, 0, :], func=ACT.Exp, bias=neg_max[:], accum_out=row_sum[:])
-        quantise_keys(1)
-        score_passes(1)
-        normalise_and_store(exps, row_sum, 0)
 
+        exps_0, row_sum_0 = exps, row_sum
         neg_max = per_group.tile([P, 1], F32, tag="neg_max")
         exps = per_group.tile([P, WINDOW_ROWS], F32, tag="exps")
         row_sum = per_group.tile([P, 1], F32, tag="row_sum")
@@ -314,6 +314,7 @@ def tile_slidingwindowattention_pa_s_kernel(tc, x, Wqk, out):
             nc.vector.tensor_reduce(
                 out=neg_max[rows], in_=group_scores[1][rows, cols], axis=AXIS_X, op=ALU.max, negate=True
             )
+        normalise_and_store(exps_0, row_sum_0, 0)
         for i in range(GROUP):
             rows = slice(QUADRANT * i, QUADRANT * (i + 1))
             cols = slice(WINDOW_ROWS * i, WINDOW_ROWS * (i + 1))

@@ -37,7 +37,8 @@ RUNS = TILES // RUN
 GROUP_RUNS = GROUP // RUN
 AHEAD = 2
 
-WARM_UPS = 5
+BANK = 512
+WARM_COLS = 384
 
 FLOPS = 2 * TOKENS * MODEL * 2 * MODEL + HEADS * 2 * WINDOW_ROWS * WINDOW_ROWS * ROW_TOKENS * HEAD_DIM
 
@@ -67,9 +68,8 @@ def tile_slidingwindowattention_pa_s_kernel(tc, x, Wqk, out):
         consts = ctx.enter_context(tc.tile_pool(name="consts", bufs=1))
         resident = ctx.enter_context(tc.tile_pool(name="resident", bufs=TILES))
         per_group = ctx.enter_context(tc.tile_pool(name="per_group", bufs=GROUPS))
-        banks = ctx.enter_context(tc.psum_pool(name="banks", bufs=4))
-        proj_banks = ctx.enter_context(tc.psum_pool(name="proj_banks", bufs=2))
-        score_banks = ctx.enter_context(tc.psum_pool(name="score_banks", bufs=1))
+        banks = ctx.enter_context(tc.psum_pool(name="banks", bufs=5))
+        proj_banks = ctx.enter_context(tc.psum_pool(name="proj_banks", bufs=3))
 
         x_rows = consts.tile([P, MODEL], BF16)
         nc.sync.dma_start(out=x_rows[:], in_=x.flatten_outer_dims())
@@ -80,10 +80,7 @@ def tile_slidingwindowattention_pa_s_kernel(tc, x, Wqk, out):
             source = Wqk[first_row : first_row + RUN * P, :].rearrange("(t p) k -> p t k", t=RUN)
             if run in (0, RUNS - 2, RUNS - 1):
                 for t in range(RUN):
-                    parts = PASSES if run * RUN + t == TILES - 1 else 1
-                    for part in range(parts):
-                        cols = slice(part * MODEL // parts, (part + 1) * MODEL // parts)
-                        nc.sync.dma_start(out=run_rows[:, t, cols], in_=source[:, t, cols])
+                    nc.sync.dma_start(out=run_rows[:, t, :], in_=source[:, t, :])
             else:
                 nc.sync.dma_start(out=run_rows[:], in_=source)
             for t in range(RUN):
@@ -92,29 +89,14 @@ def tile_slidingwindowattention_pa_s_kernel(tc, x, Wqk, out):
         warm = consts.tile([P, 1], F32)
         nc.vector.memset(warm[:], 0.0)
         nc.scalar.activation(out=warm[:], in_=warm[:], func=ACT.Exp)
-        zeros = consts.tile([P, P], F32)
+        zeros = consts.tile([P, WARM_COLS], F32)
         nc.vector.memset(zeros[:], 0.0)
-        scores_0 = score_banks.tile([P, 2 * OWN], F32)
-        scores_1 = score_banks.tile([P, 512], F32)
-        group_scores = [scores_0[:], scores_1[:, : 2 * OWN]]
-        unread = scores_1[:, 2 * OWN : 2 * OWN + PASSES * TOKENS]
+        unread = proj_banks.tile([P, BANK], F32, tag="proj")
+        nc.tensor.matmul(out=unread[:, :WARM_COLS], lhsT=zeros[:, :P], rhs=zeros[:], start=True, stop=True)
 
-        def keep_clock_plain():
-            nc.tensor.matmul(out=unread[:, :P], lhsT=zeros[:], rhs=zeros[:], start=True, stop=True)
+        def keep_clock():
+            nc.tensor.matmul(out=unread[:, :P], lhsT=zeros[:, :P], rhs=zeros[:, :P], start=True, stop=True)
 
-        def keep_clock_mx(j):
-            nc.tensor.matmul_mx(
-                out=unread,
-                lhsT=w_parts[j][0][0].bitcast(FP8X4),
-                lhsT_scale=w_parts[j][0][1],
-                rhs=x_codes[:].bitcast(FP8X4),
-                rhs_scale=x_scales[:],
-                start=True,
-                stop=True,
-            )
-
-        for i in range(WARM_UPS):
-            keep_clock_plain()
         identity = consts.tile([P, P], F32)
         make_identity(nc, identity[:])
         token_order = consts.tile([P, P], F32)
@@ -137,8 +119,8 @@ def tile_slidingwindowattention_pa_s_kernel(tc, x, Wqk, out):
             q_scales.append(scales)
             codes = per_group.tile([P, (TOKEN_PASSES + 1) * OWN], U32, align_bytes=64, tag="k_codes")
             scales = per_group.tile([P, (TOKEN_PASSES + 1) * OWN], U8, align_bytes=64, tag="k_scales")
-            nc.gpsimd.memset(codes[:, TOKEN_PASSES * OWN :].bitcast(I32), 0)
-            nc.gpsimd.memset(scales[:, TOKEN_PASSES * OWN :].bitcast(I32), 0)
+            nc.vector.memset(codes[:, TOKEN_PASSES * OWN :].bitcast(I32), 0)
+            nc.vector.memset(scales[:, TOKEN_PASSES * OWN :].bitcast(I32), 0)
             k_codes.append(codes)
             k_scales.append(scales)
             values = per_group.tile([P, TOKEN_PASSES, GROUP, COLS], BF16, align_bytes=64, tag="q_values")
@@ -147,7 +129,6 @@ def tile_slidingwindowattention_pa_s_kernel(tc, x, Wqk, out):
             k_values.append(values)
 
         x_flipped = flip_rows(nc, banks, x_rows[:], token_order)
-        keep_clock_plain()
         x_grouped = consts.tile([P, PASSES, TOKENS, PACK], BF16, align_bytes=64)
         nc.scalar.copy(
             out=x_grouped[:].bitcast(F32), in_=x_flipped.rearrange("p g u n -> p g n u")
@@ -175,20 +156,22 @@ def tile_slidingwindowattention_pa_s_kernel(tc, x, Wqk, out):
             )
 
         def project(tiles):
-            proj = proj_banks.tile([P, RUN, TOKEN_PASSES, COLS], F32)
+            proj = proj_banks.tile([P, BANK], F32)
             for i, j in enumerate(tiles):
                 for g in range(PASSES):
                     codes, scales = w_parts[j][g]
                     nc.tensor.matmul_mx(
-                        out=proj[:, i, :, :].rearrange("p r n -> p (r n)"),
+                        out=proj[:, i * TOKENS : (i + 1) * TOKENS],
                         lhsT=codes.bitcast(FP8X4),
                         lhsT_scale=scales,
-                        rhs=x_codes[:, g * P : (g + 1) * P].bitcast(FP8X4),
-                        rhs_scale=x_scales[:, g * P : (g + 1) * P],
+                        rhs=x_codes[:, g * TOKENS : (g + 1) * TOKENS].bitcast(FP8X4),
+                        rhs_scale=x_scales[:, g * TOKENS : (g + 1) * TOKENS],
                         start=(g == 0),
                         stop=(g == PASSES - 1),
                     )
-            by_pass = proj[:, : len(tiles)].rearrange("p i r n -> p r i n")
+            by_pass = proj[:, : len(tiles) * TOKENS].rearrange(
+                "p (i r n) -> p r i n", r=TOKEN_PASSES, n=COLS
+            )
             is_key, pair = divmod(tiles[0], PAIRS)
             a, first = divmod(pair, GROUP)
             pairs = slice(first, first + len(tiles))
@@ -220,13 +203,15 @@ def tile_slidingwindowattention_pa_s_kernel(tc, x, Wqk, out):
             )
 
         scores = consts.tile([P, 1, WINDOW_ROWS], F32)
+        score_tiles = []
 
         def score_passes(a):
+            group_scores = proj_banks.tile([P, BANK], F32, tag="proj")
             for r in range(TOKEN_PASSES):
                 span = slice(r * OWN, (r + 2) * OWN)
                 rows = slice(r * GROUP, (r + 1) * GROUP)
                 nc.tensor.matmul_mx(
-                    out=group_scores[a],
+                    out=group_scores[:, : 2 * OWN],
                     lhsT=q_codes[a][:, rows].rearrange("p c e w -> p (c e w)").bitcast(FP8X4),
                     lhsT_scale=q_scales[a][:, rows].rearrange("p c e w -> p (c e w)"),
                     rhs=k_codes[a][:, span].bitcast(FP8X4),
@@ -234,12 +219,13 @@ def tile_slidingwindowattention_pa_s_kernel(tc, x, Wqk, out):
                     start=(r == 0),
                     stop=(r == TOKEN_PASSES - 1),
                 )
+            score_tiles.append(group_scores)
 
         def pick_own(a):
             for i in range(GROUP):
                 rows = slice(QUADRANT * i, QUADRANT * (i + 1))
                 cols = slice(WINDOW_ROWS * i, WINDOW_ROWS * (i + 1))
-                nc.vector.tensor_copy(out=scores[rows, a, :], in_=group_scores[a][rows, cols])
+                nc.vector.tensor_copy(out=scores[rows, a, :], in_=score_tiles[a][rows, cols])
 
         def normalise_and_store(exps, row_sum, a):
             inverse = per_group.tile([P, 1], F32, tag="inverse")
@@ -253,8 +239,8 @@ def tile_slidingwindowattention_pa_s_kernel(tc, x, Wqk, out):
             tiles = range(step * RUN, (step + 1) * RUN)
             for j in tiles:
                 w_flipped.append(flip_rows(nc, banks, w_rows[j], identity))
-            if step < AHEAD:
-                keep_clock_plain()
+                if j in (0, 1, 3):
+                    keep_clock()
             for j in tiles:
                 regroup(j)
                 if j > 0:
@@ -264,7 +250,6 @@ def tile_slidingwindowattention_pa_s_kernel(tc, x, Wqk, out):
             if step >= AHEAD:
                 first = (step - AHEAD) * RUN
                 project([first, first + 1])
-                keep_clock_mx(first)
 
         project([LAST - 5, LAST - 4])
         w_flipped.append(flip_rows(nc, banks, w_rows[LAST - 1], identity))
@@ -312,7 +297,7 @@ def tile_slidingwindowattention_pa_s_kernel(tc, x, Wqk, out):
             rows = slice(QUADRANT * i, QUADRANT * (i + 1))
             cols = slice(WINDOW_ROWS * i, WINDOW_ROWS * (i + 1))
             nc.vector.tensor_reduce(
-                out=neg_max[rows], in_=group_scores[1][rows, cols], axis=AXIS_X, op=ALU.max, negate=True
+                out=neg_max[rows], in_=score_tiles[1][rows, cols], axis=AXIS_X, op=ALU.max, negate=True
             )
         normalise_and_store(exps_0, row_sum_0, 0)
         for i in range(GROUP):
@@ -320,7 +305,7 @@ def tile_slidingwindowattention_pa_s_kernel(tc, x, Wqk, out):
             cols = slice(WINDOW_ROWS * i, WINDOW_ROWS * (i + 1))
             nc.scalar.activation(
                 out=exps[rows],
-                in_=group_scores[1][rows, cols],
+                in_=score_tiles[1][rows, cols],
                 func=ACT.Exp,
                 bias=neg_max[rows],
                 accum_out=row_sum[rows],

from contextlib import ExitStack

import concourse.mybir as mybir
from concourse.masks import make_identity

F32 = mybir.dt.float32
BF16 = mybir.dt.bfloat16
I32 = mybir.dt.int32
U32 = mybir.dt.uint32
U8 = mybir.dt.uint8
FP8X4 = mybir.dt.float8_e4m3fn_x4
ALU = mybir.AluOpType
ACT = mybir.ActivationFunctionType
AXIS_X = mybir.AxisListType.X

P = 128
PACK = 4
TOKENS = 128
MODEL = 1024
HEADS = 16
HEAD_DIM = 64
WINDOW_ROWS = 16
ROW_TOKENS = TOKENS // WINDOW_ROWS

PASSES = MODEL // (P * PACK)
HALVES = 2
PAIRS = HEADS // 2
TOKEN_PASSES = ROW_TOKENS // PACK
COLS = WINDOW_ROWS * PACK
QUADRANT = 32
GROUP = P // QUADRANT
GROUPS = PAIRS // GROUP
OWN = GROUP * WINDOW_ROWS
RUN = 2
TILES = 2 * PAIRS
RUNS = TILES // RUN
GROUP_RUNS = GROUP // RUN
AHEAD = 2

BANK = 512
WARM_COLS = 384

FLOPS = 2 * TOKENS * MODEL * 2 * MODEL + HEADS * 2 * WINDOW_ROWS * WINDOW_ROWS * ROW_TOKENS * HEAD_DIM


def flip_rows(nc, banks, rows, order):
    words = rows.bitcast(F32)
    passes = words.shape[1] // (HALVES * P)
    flipped = banks.tile([P, passes, HALVES, P], F32, tag="flipped")
    for g in range(passes):
        for u in range(HALVES):
            first = (g * HALVES + u) * P
            nc.tensor.transpose(flipped[:, g, u, :], words[:, first : first + P], order[:])
    return flipped[:]


def quantise(nc, pool, name, grouped, columns):
    codes = pool.tile([P, columns], U32, align_bytes=64, tag=name + "_codes")
    scales = pool.tile([P, columns], U8, align_bytes=64, tag=name + "_scales")
    nc.vector.quantize_mx(out=codes[:].bitcast(FP8X4), scales=scales[:], in_=grouped)
    return codes, scales


def tile_slidingwindowattention_pa_s_kernel(tc, x, Wqk, out):
    nc = tc.nc
    with ExitStack() as ctx:
        ctx.enter_context(tc.manual_schedule())
        consts = ctx.enter_context(tc.tile_pool(name="consts", bufs=1))
        resident = ctx.enter_context(tc.tile_pool(name="resident", bufs=TILES))
        per_group = ctx.enter_context(tc.tile_pool(name="per_group", bufs=GROUPS))
        banks = ctx.enter_context(tc.psum_pool(name="banks", bufs=5))
        proj_banks = ctx.enter_context(tc.psum_pool(name="proj_banks", bufs=3))

        x_rows = consts.tile([P, MODEL], BF16)
        nc.sync.dma_start(out=x_rows[:], in_=x.flatten_outer_dims())
        w_rows = []
        for run in range(RUNS):
            first_row = run * RUN * P
            run_rows = resident.tile([P, RUN, MODEL], BF16)
            source = Wqk[first_row : first_row + RUN * P, :].rearrange("(t p) k -> p t k", t=RUN)
            if run in (0, RUNS - 2, RUNS - 1):
                for t in range(RUN):
                    nc.sync.dma_start(out=run_rows[:, t, :], in_=source[:, t, :])
            else:
                nc.sync.dma_start(out=run_rows[:], in_=source)
            for t in range(RUN):
                w_rows.append(run_rows[:, t, :])

        warm = consts.tile([P, 1], F32)
        nc.vector.memset(warm[:], 0.0)
        nc.scalar.activation(out=warm[:], in_=warm[:], func=ACT.Exp)
        zeros = consts.tile([P, WARM_COLS], F32)
        nc.vector.memset(zeros[:], 0.0)
        unread = proj_banks.tile([P, BANK], F32, tag="proj")
        nc.tensor.matmul(out=unread[:, :WARM_COLS], lhsT=zeros[:, :P], rhs=zeros[:], start=True, stop=True)

        def keep_clock():
            nc.tensor.matmul(out=unread[:, :P], lhsT=zeros[:, :P], rhs=zeros[:, :P], start=True, stop=True)

        identity = consts.tile([P, P], F32)
        make_identity(nc, identity[:])
        token_order = consts.tile([P, P], F32)
        nc.vector.tensor_copy(
            out=token_order[:].rearrange("p (r w t) -> p r w t", r=TOKEN_PASSES, w=WINDOW_ROWS),
            in_=identity[:].rearrange("p (w r t) -> p r w t", w=WINDOW_ROWS, r=TOKEN_PASSES),
        )

        q_codes = []
        q_scales = []
        k_codes = []
        k_scales = []
        q_values = []
        k_values = []
        for a in range(GROUPS):
            codes = per_group.tile([P, TOKEN_PASSES * GROUP, 2, WINDOW_ROWS], U32, align_bytes=64, tag="qp_codes")
            nc.gpsimd.memset(codes[:].rearrange("p c e w -> p (c e w)").bitcast(I32), 0)
            q_codes.append(codes)
            scales = per_group.tile([P, TOKEN_PASSES * GROUP, 2, WINDOW_ROWS], U8, align_bytes=64, tag="qp_scales")
            q_scales.append(scales)
            codes = per_group.tile([P, (TOKEN_PASSES + 1) * OWN], U32, align_bytes=64, tag="k_codes")
            scales = per_group.tile([P, (TOKEN_PASSES + 1) * OWN], U8, align_bytes=64, tag="k_scales")
            nc.vector.memset(codes[:, TOKEN_PASSES * OWN :].bitcast(I32), 0)
            nc.vector.memset(scales[:, TOKEN_PASSES * OWN :].bitcast(I32), 0)
            k_codes.append(codes)
            k_scales.append(scales)
            values = per_group.tile([P, TOKEN_PASSES, GROUP, COLS], BF16, align_bytes=64, tag="q_values")
            q_values.append(values)
            values = per_group.tile([P, TOKEN_PASSES, GROUP, COLS], BF16, align_bytes=64, tag="k_values")
            k_values.append(values)

        x_flipped = flip_rows(nc, banks, x_rows[:], token_order)
        x_grouped = consts.tile([P, PASSES, TOKENS, PACK], BF16, align_bytes=64)
        nc.scalar.copy(
            out=x_grouped[:].bitcast(F32), in_=x_flipped.rearrange("p g u n -> p g n u")
        )
        x_codes, x_scales = quantise(
            nc, consts, "x", x_grouped[:].rearrange("p g n t -> p (g n t)"), PASSES * TOKENS
        )

        w_flipped = []
        w_grouped = []
        w_parts = []

        def regroup(j):
            grouped = resident.tile([P, PASSES, P, PACK], BF16, align_bytes=64)
            copy = nc.vector.tensor_copy if j in (1, 4, 7) else nc.scalar.copy
            copy(out=grouped[:].bitcast(F32), in_=w_flipped[j].rearrange("p g u m -> p g m u"))
            w_grouped.append(grouped)

        def quantise_tile(j):
            codes, scales = quantise(
                nc, resident, "w", w_grouped[j][:].rearrange("p g m t -> p (g m t)"), PASSES * P
            )
            w_parts.append(
                [(codes[:, g * P : (g + 1) * P], scales[:, g * P : (g + 1) * P]) for g in range(PASSES)]
            )

        def project(tiles):
            proj = proj_banks.tile([P, BANK], F32)
            for i, j in enumerate(tiles):
                for g in range(PASSES):
                    codes, scales = w_parts[j][g]
                    nc.tensor.matmul_mx(
                        out=proj[:, i * TOKENS : (i + 1) * TOKENS],
                        lhsT=codes.bitcast(FP8X4),
                        lhsT_scale=scales,
                        rhs=x_codes[:, g * TOKENS : (g + 1) * TOKENS].bitcast(FP8X4),
                        rhs_scale=x_scales[:, g * TOKENS : (g + 1) * TOKENS],
                        start=(g == 0),
                        stop=(g == PASSES - 1),
                    )
            by_pass = proj[:, : len(tiles) * TOKENS].rearrange(
                "p (i r n) -> p r i n", r=TOKEN_PASSES, n=COLS
            )
            is_key, pair = divmod(tiles[0], PAIRS)
            a, first = divmod(pair, GROUP)
            pairs = slice(first, first + len(tiles))
            if is_key:
                nc.scalar.copy(out=k_values[a][:, :, pairs, :], in_=by_pass)
            else:
                nc.scalar.mul(q_values[a][:, :, pairs, :], by_pass, HEAD_DIM**-0.5)

        def quantise_queries(a):
            codes, scales = quantise(
                nc, per_group, "q", q_values[a][:].rearrange("p r i n -> p (r i n)"), TOKEN_PASSES * OWN
            )
            for e in range(2):
                head = slice(HEAD_DIM * e, HEAD_DIM * (e + 1))
                nc.vector.tensor_copy(
                    out=q_codes[a][head, :, e, :].bitcast(I32),
                    in_=codes[head].rearrange("p (c w) -> p c w", w=WINDOW_ROWS).bitcast(I32),
                )
                nc.vector.tensor_copy(
                    out=q_scales[a][:, :, e, :],
                    in_=scales[:].rearrange("p (c w) -> p c w", w=WINDOW_ROWS),
                )

        def quantise_keys(a):
            nc.vector.quantize_mx(
                out=k_codes[a][:, : TOKEN_PASSES * OWN].bitcast(FP8X4),
                scales=k_scales[a][:, : TOKEN_PASSES * OWN],
                in_=k_values[a][:].rearrange("p r i n -> p (r i n)"),
            )

        scores = consts.tile([P, 1, WINDOW_ROWS], F32)
        score_tiles = []

        def score_passes(a):
            group_scores = proj_banks.tile([P, BANK], F32, tag="proj")
            for r in range(TOKEN_PASSES):
                span = slice(r * OWN, (r + 2) * OWN)
                rows = slice(r * GROUP, (r + 1) * GROUP)
                nc.tensor.matmul_mx(
                    out=group_scores[:, : 2 * OWN],
                    lhsT=q_codes[a][:, rows].rearrange("p c e w -> p (c e w)").bitcast(FP8X4),
                    lhsT_scale=q_scales[a][:, rows].rearrange("p c e w -> p (c e w)"),
                    rhs=k_codes[a][:, span].bitcast(FP8X4),
                    rhs_scale=k_scales[a][:, span],
                    start=(r == 0),
                    stop=(r == TOKEN_PASSES - 1),
                )
            score_tiles.append(group_scores)

        def pick_own(a):
            for i in range(GROUP):
                rows = slice(QUADRANT * i, QUADRANT * (i + 1))
                cols = slice(WINDOW_ROWS * i, WINDOW_ROWS * (i + 1))
                nc.vector.tensor_copy(out=scores[rows, a, :], in_=score_tiles[a][rows, cols])

        def normalise_and_store(exps, row_sum, a):
            inverse = per_group.tile([P, 1], F32, tag="inverse")
            nc.vector.reciprocal(out=inverse[:], in_=row_sum[:])
            weights = per_group.tile([P, WINDOW_ROWS], F32, tag="weights")
            nc.vector.tensor_scalar_mul(out=weights[:], in0=exps[:], scalar1=inverse[:])
            nc.sync.dma_start(out=out.flatten_outer_dims()[a * P : (a + 1) * P, :], in_=weights[:])

        LAST = TILES - 1
        for step in range(RUNS - 1):
            tiles = range(step * RUN, (step + 1) * RUN)
            for j in tiles:
                w_flipped.append(flip_rows(nc, banks, w_rows[j], identity))
                if j in (0, 1, 3):
                    keep_clock()
            for j in tiles:
                regroup(j)
                if j > 0:
                    quantise_tile(j - 1)
            if step == AHEAD + GROUP_RUNS:
                quantise_queries(0)
            if step >= AHEAD:
                first = (step - AHEAD) * RUN
                project([first, first + 1])

        project([LAST - 5, LAST - 4])
        w_flipped.append(flip_rows(nc, banks, w_rows[LAST - 1], identity))
        halves = []
        for g in range(PASSES):
            cols = slice(g * MODEL // PASSES, (g + 1) * MODEL // PASSES)
            halves.append(flip_rows(nc, banks, w_rows[LAST][:, cols], identity))
        quantise_tile(LAST - 2)
        quantise_keys(0)
        regroup(LAST - 1)
        half_grouped = []
        for g in range(PASSES):
            grouped = per_group.tile([P, P, PACK], BF16, align_bytes=64, tag="half_grouped")
            copy = nc.vector.tensor_copy if g == 1 else nc.scalar.copy
            copy(out=grouped[:].bitcast(F32), in_=halves[g].rearrange("p o u m -> p (o m) u"))
            half_grouped.append(grouped)
        project([LAST - 3, LAST - 2])
        quantise_tile(LAST - 1)
        parts = []
        for g in range(PASSES):
            codes, scales = quantise(
                nc, per_group, "half", half_grouped[g][:].rearrange("p m t -> p (m t)"), P
            )
            parts.append((codes[:], scales[:]))
        w_parts.append(parts)
        project([LAST - 1])
        project([LAST])
        quantise_queries(1)
        score_passes(0)
        quantise_keys(1)
        score_passes(1)

        pick_own(0)
        neg_max = per_group.tile([P, 1], F32, tag="neg_max")
        nc.vector.tensor_reduce(out=neg_max[:], in_=scores[:, 0, :], axis=AXIS_X, op=ALU.max, negate=True)
        exps = per_group.tile([P, WINDOW_ROWS], F32, tag="exps")
        row_sum = per_group.tile([P, 1], F32, tag="row_sum")
        nc.scalar.activation(out=exps[:], in_=scores[:, 0, :], func=ACT.Exp, bias=neg_max[:], accum_out=row_sum[:])

        exps_0, row_sum_0 = exps, row_sum
        neg_max = per_group.tile([P, 1], F32, tag="neg_max")
        exps = per_group.tile([P, WINDOW_ROWS], F32, tag="exps")
        row_sum = per_group.tile([P, 1], F32, tag="row_sum")
        for i in range(GROUP):
            rows = slice(QUADRANT * i, QUADRANT * (i + 1))
            cols = slice(WINDOW_ROWS * i, WINDOW_ROWS * (i + 1))
            nc.vector.tensor_reduce(
                out=neg_max[rows], in_=score_tiles[1][rows, cols], axis=AXIS_X, op=ALU.max, negate=True
            )
        normalise_and_store(exps_0, row_sum_0, 0)
        for i in range(GROUP):
            rows = slice(QUADRANT * i, QUADRANT * (i + 1))
            cols = slice(WINDOW_ROWS * i, WINDOW_ROWS * (i + 1))
            nc.scalar.activation(
                out=exps[rows],
                in_=score_tiles[1][rows, cols],
                func=ACT.Exp,
                bias=neg_max[rows],
                accum_out=row_sum[rows],
            )
        normalise_and_store(exps, row_sum, 1)
